import numpy as np
import ml_dtypes


def mxq(x, axis, fmt="e4m3"):
    dtype, down = {"e4m3": (ml_dtypes.float8_e4m3fn, 7), "e5m2": (ml_dtypes.float8_e5m2, 14)}[fmt]
    v = np.moveaxis(np.asarray(x, np.float32).astype(ml_dtypes.bfloat16).astype(np.float64), axis, -1)
    blocks = v.reshape(v.shape[:-1] + (-1, 32))
    amax = np.abs(blocks).max(-1, keepdims=True)
    byte = np.maximum(np.where(amax > 0, np.frexp(amax)[1] - 1 + 127, 0) - down, 1)
    scale = np.exp2(byte - 127.0)
    codes = (blocks / scale).astype(np.float32).astype(dtype).astype(np.float64)
    return np.moveaxis((codes * scale).reshape(v.shape), -1, axis)


WIDE = False


def mx_kscale(k):
    if not WIDE:
        return np.ones(k)
    levels = np.array([10, -10, 5, -5, 0])
    if k % 512:
        return np.exp2(np.random.permutation(np.resize(levels, k // 32))).repeat(32)
    a = np.empty((k // 512, 16))
    for p in range(k // 512):
        a[p, :8] = np.random.permutation(np.resize(levels, 8))
        for g in range(8):
            far = levels[np.abs(levels - a[p, g]) >= 10]
            a[p, g + 8] = far[np.random.randint(len(far))]
    return np.exp2(a.ravel()).repeat(32)


BF16 = ml_dtypes.bfloat16


def bf(x):
    return np.asarray(x, np.float32).astype(BF16)


def f64(x):
    return np.asarray(x).astype(np.float64)


E2M1 = np.array([0.0, 0.5, 1.0, 1.5, 2.0, 3.0, 4.0, 6.0, -0.0, -0.5, -1.0, -1.5, -2.0, -3.0, -4.0, -6.0])


def pack_weight(w, fmt):
    k, n = w.shape
    w = f64(bf(w)).reshape(k // 32, 32, n)
    amax = np.abs(w).max(1)
    if fmt == "e4m3":
        byte = np.frexp(amax)[1] - 1 + 127 - 7
    else:
        mant, ex = np.frexp(amax / 6.0)
        byte = np.where(mant > 0.5, ex, ex - 1) + 127
    byte = np.clip(np.where(amax > 0, byte, 1), 1, 254)
    scaled = (w * np.exp2(127.0 - byte)[:, None, :]).reshape(k, n).astype(np.float32)
    by_word = np.ascontiguousarray(scaled.reshape(k // 512, 128, 4, n).transpose(0, 1, 3, 2))
    if fmt == "e4m3":
        words = by_word.astype(ml_dtypes.float8_e4m3fn).view(np.uint8)
    else:
        c = by_word.astype(ml_dtypes.float4_e2m1fn).view(np.uint8) & 0xF
        words = c[..., 0::2] | (c[..., 1::2] << 4)
    return np.ascontiguousarray(words), np.ascontiguousarray(byte.astype(np.uint8).reshape(k // 512, 16, n))


def unpack_weight(words, scales, fmt):
    g, p, n, _ = words.shape
    if fmt == "e4m3":
        vals = np.ascontiguousarray(words).view(ml_dtypes.float8_e4m3fn).astype(np.float64)
    else:
        nib = np.empty((g, p, n, 4), np.uint8)
        nib[..., 0::2] = words & 0xF
        nib[..., 1::2] = words >> 4
        vals = E2M1[nib]
    vals = vals * np.repeat(np.exp2(scales.astype(np.float64) - 127.0), 8, axis=1)[..., None]
    return vals.transpose(0, 1, 3, 2).reshape(g * 512, n)
def pack4(w):
    words, scales = pack_weight(w, "e2m1")
    return words.reshape(words.shape[0], 128, -1), scales


def unpack4(words, scales):
    return unpack_weight(words.reshape(words.shape[0], 128, -1, 2), scales, "e2m1")


B, H, W, D, Dh, Dq, R, T = 16, 16, 16, 512, 512, 128, 16, 8
EPS = 1e-6


def layer_norm(v, g, b):
    mu = v.mean(-1, keepdims=True)
    var = ((v - mu) ** 2).mean(-1, keepdims=True)
    return (v - mu) / np.sqrt(var + EPS) * g + b


def draw0():
    rn = np.random.standard_normal
    s, t = mx_kscale(D), mx_kscale(Dh)
    x = bf(rn((B, H, W, D)) * s)
    z2 = bf(rn((B, H, W, Dq)) * 1.5)
    U1_w_words, U1_w_scales = pack4((rn((Dh, D)) * np.sqrt(2.0 / D) / s).T)
    U1_b = bf(rn(Dh) * 0.5)
    U3_w = bf(rn((Dh, Dq)) * np.sqrt(2.0 / Dq))
    U3_b = bf(rn(Dh) * 0.5)
    C_w_words, C_w_scales = pack4((rn((D, Dh)) / np.sqrt(Dh) / t).T)
    return {
        "x": x,
        "z2": z2,
        "U1_w_words": U1_w_words,
        "U1_w_scales": U1_w_scales,
        "U1_b": U1_b,
        "U3_w": U3_w,
        "U3_b": U3_b,
        "C_w_words": C_w_words,
        "C_w_scales": C_w_scales,
        "C_b": bf(rn(D) * 0.3),
        "ln1_g": bf((1.0 + 0.1 * rn(Dh)) * t),
        "ln1_b": bf(0.2 * rn(Dh) * t),
        "ln3_g": bf(1.0 + 0.1 * rn(Dh)),
        "ln3_b": bf(0.2 * rn(Dh)),
        "alpha": bf(0.6 + 0.2 * np.random.random(1)),
    }


def core(x, z2, U1_w_words, U1_w_scales, U1_b, U3_w, U3_b, C_w_words, C_w_scales, C_b, ln1_g, ln1_b, ln3_g, ln3_b, alpha):
    out1 = (mxq(f64(x), 3, "e4m3") @ unpack4(U1_w_words, U1_w_scales)) + f64(U1_b)
    out3 = f64(z2) @ f64(U3_w).T + f64(U3_b)
    o1 = layer_norm(out1, f64(ln1_g), f64(ln1_b))
    o3 = layer_norm(out3, f64(ln3_g), f64(ln3_b))
    h = o1 + f64(alpha) * (o1 * o3)
    return (mxq(h, 3, "e4m3") @ unpack4(C_w_words, C_w_scales)) + f64(C_b)


def e4m3fn_bytes(y):
    return np.clip(np.asarray(y, np.float64), -448.0, 448.0).astype(np.float32).astype(ml_dtypes.float8_e4m3fn).view(np.uint8)


def e4m3fn_values(b):
    return np.asarray(b, np.uint8).view(ml_dtypes.float8_e4m3fn).astype(np.float64)


def setup_inputs():
    d = draw0()
    x0 = np.asarray(d['x']).astype(np.float64)
    s = (np.max(np.abs(x0), axis=(0, 1, 2), keepdims=True) / 448.0).astype(np.float32)
    out = {}
    for k, v in d.items():
        if k == 'x':
            out['x_bytes'] = e4m3fn_bytes(x0 / s.astype(np.float64))
            out['x_scale'] = s
        else:
            out[k] = v
    return out


def reference(x_bytes, x_scale, z2, U1_w_words, U1_w_scales, U1_b, U3_w, U3_b, C_w_words, C_w_scales, C_b, ln1_g, ln1_b, ln3_g, ln3_b, alpha):
    return core(e4m3fn_values(x_bytes) * x_scale.astype(np.float64), z2, U1_w_words, U1_w_scales, U1_b, U3_w, U3_b, C_w_words, C_w_scales, C_b, ln1_g, ln1_b, ln3_g, ln3_b, alpha)

from contextlib import ExitStack

import concourse.mybir as mybir
from concourse.masks import make_identity

F32 = mybir.dt.float32
BF16 = mybir.dt.bfloat16
U32 = mybir.dt.uint32
I32 = mybir.dt.int32
U8 = mybir.dt.uint8
FP8 = mybir.dt.float8_e4m3fn
FP8X4 = mybir.dt.float8_e4m3fn_x4
FP4X4 = mybir.dt.float4_e2m1fn_x4
ALU = mybir.AluOpType
ACT = mybir.ActivationFunctionType
AX = mybir.AxisListType

P = 128
D = 512
DQ = 128
TOKENS = 4096
JT = 4
GT = 2
NT = TOKENS // P
EPS = 1e-6
FLOPS = 2 * TOKENS * D * (D + D + DQ)


def tile_polymlp_skiplora_pa_t_w4_kernel(
    tc, x_bytes, x_scale, z2, u1_words, u1_scales, u1_b, u3_w, u3_b, c_words, c_scales, c_b,
    ln1_g, ln1_b, ln3_g, ln3_b, alpha, out,
):
    nc = tc.nc
    xv = x_bytes.rearrange("b h w d -> (b h w) d").rearrange("(g p j) d -> g p (j d)", p=P, j=JT)
    zv = z2.rearrange("b h w d -> (b h w) d").rearrange("(g p j) d -> g p (j d)", p=P, j=JT)
    ov = out.rearrange("b h w d -> (b h w) d").rearrange("(g p j) d -> g p (j d)", p=P, j=JT)

    with ExitStack() as ctx:
        keep = ctx.enter_context(tc.tile_pool(name="keep", bufs=1))
        tmp = ctx.enter_context(tc.tile_pool(name="tmp", bufs=1))
        sb = ctx.enter_context(tc.tile_pool(name="sb", bufs=2))
        ps_x = ctx.enter_context(tc.psum_pool(name="ps_x", bufs=1))
        ps_m = ctx.enter_context(tc.psum_pool(name="ps_m", bufs=2))
        ps_3 = ctx.enter_context(tc.psum_pool(name="ps_3", bufs=3))
        ps_a = ctx.enter_context(tc.psum_pool(name="ps_a", bufs=1))
        ps_b = ctx.enter_context(tc.psum_pool(name="ps_b", bufs=1))

        eps = keep.tile([P, 1], F32, name="eps")
        nc.vector.memset(eps[:], EPS)
        one = keep.tile([P, 1], F32, name="one")
        nc.vector.memset(one[:], 1.0)
        warm = keep.tile([P, 1], F32, name="warm")
        nc.scalar.activation(out=warm[:], in_=one[:], func=ACT.Sqrt)

        ident = keep.tile([P, P], F32, name="ident")
        make_identity(nc, ident[:])
        ident_b = keep.tile([P, P], BF16, name="ident_b")
        nc.gpsimd.tensor_copy(out=ident_b[:], in_=ident[:])

        state = {}

        def load(g):
            xb = sb.tile([P, JT * D], U8, tag="xb", name="xb", bufs=3)
            nc.sync.dma_start(out=xb[:], in_=xv[g])
            state["xb", g] = xb

        def loadz(g):
            zb = sb.tile([P, JT * DQ], BF16, tag="zb", name="zb", bufs=3)
            nc.sync.dma_start(out=zb[:], in_=zv[g])
            state["zb", g] = zb

        load(0)
        w1_raw = tmp.tile([P, 2 * D], U8, name="w1_raw")
        nc.sync.dma_start(out=w1_raw[:], in_=u1_words[0])
        xs_col = tmp.tile([P, 4], F32, name="xs_col")
        nc.scalar.dma_start(out=xs_col[:], in_=x_scale.rearrange("a b c (p t) -> p (a b c t)", t=4))

        def load_col(vec, name):
            raw = tmp.tile([P, 4], BF16, name=name)
            nc.scalar.dma_start(out=raw[:], in_=vec.rearrange("(p t) -> p t", t=4))
            return raw

        b1_r = load_col(u1_b, "b1_r")
        u3_r = tmp.tile([P, 4, DQ], BF16, name="u3_r")
        nc.scalar.dma_start(out=u3_r[:], in_=u3_w.rearrange("(m t) q -> m t q", t=4))
        b3_r = load_col(u3_b, "b3_r")
        g1_r = load_col(ln1_g, "g1_r")
        e1_r = load_col(ln1_b, "e1_r")
        g3_r = load_col(ln3_g, "g3_r")
        e3_r = load_col(ln3_b, "e3_r")
        al_r = tmp.tile([P, 1], BF16, name="al_r")
        nc.scalar.dma_start(out=al_r[:], in_=alpha.partition_broadcast(P))
        cb_r = load_col(c_b, "cb_r")

        w1s_raw = tmp.tile([P, D], U8, name="w1s_raw")
        nc.vector.memset(w1s_raw[:].bitcast(I32), 0)
        cws = keep.tile([P, D], U8, name="cws", align_bytes=64)
        nc.vector.memset(cws[:].bitcast(I32), 0)
        for q in range(4):
            nc.sync.dma_start(
                out=w1s_raw[32 * q : 32 * q + 4, :].bitcast(I32),
                in_=u1_scales[0][4 * q : 4 * q + 4, :].bitcast(I32),
            )
        loadz(0)
        cw = keep.tile([P, 2 * D], U8, name="cw", align_bytes=64)
        load(1)
        nc.sync.dma_start(out=cw[:], in_=c_words[0])
        for q in range(4):
            nc.sync.dma_start(
                out=cws[32 * q : 32 * q + 4, :].bitcast(I32),
                in_=c_scales[0][4 * q : 4 * q + 4, :].bitcast(I32),
            )
        loadz(1)

        def spread(col, pool, tag):
            ps = pool.tile([P, D], F32, tag=tag, name="spread")
            for t in range(4):
                nc.tensor.transpose(ps[:, t * P : (t + 1) * P], col[:, t : t + 1].to_broadcast([P, P]), ident[:])
            return ps

        xs_ps = spread(xs_col, ps_3, "m3")
        xscale = keep.tile([P, D], F32, name="xscale")
        nc.scalar.copy(out=xscale[:].rearrange("p (m t) -> p m t", t=4), in_=xs_ps[:].rearrange("p (t m) -> p m t", t=4))

        w1 = keep.tile([P, 2 * D], U8, name="w1", align_bytes=64)
        nc.vector.tensor_copy(
            out=w1[:].rearrange("p (t m b) -> p m t b", t=4, b=2),
            in_=w1_raw[:].rearrange("p (m t b) -> p m t b", t=4, b=2),
        )
        w1s = keep.tile([P, D], U8, name="w1s", align_bytes=64)
        nc.vector.tensor_copy(
            out=w1s[:].rearrange("p (t m) -> p m t", t=4),
            in_=w1s_raw[:].rearrange("p (m t) -> p m t", t=4),
        )

        b1_c = tmp.tile([P, 4], F32, name="b1_c")
        nc.vector.tensor_copy(out=b1_c[:], in_=b1_r[:])
        b1_ps = spread(b1_c, ps_3, "m3")
        b1 = keep.tile([P, D], F32, name="b1")
        nc.scalar.copy(out=b1[:], in_=b1_ps[:])

        u3_ps = ps_a.tile([P, D], BF16, tag="a", name="u3_ps")
        for t in range(4):
            nc.tensor.transpose(u3_ps[:, t * P : (t + 1) * P], u3_r[:, t, :], ident_b[:])
        u3t = keep.tile([P, D], BF16, name="u3t")
        nc.scalar.copy(out=u3t[:], in_=u3_ps[:])
        mean_w = tmp.tile([P, 4], BF16, name="mean_w")
        nc.gpsimd.memset(mean_w[:], -1.0 / D)
        mean_f = tmp.tile([P, P], F32, name="mean_f")
        nc.gpsimd.memset(mean_f[:], -1.0 / D)
        wm_ps = ps_b.tile([P, 4], F32, tag="b", name="wm_ps")
        for t in range(4):
            nc.tensor.matmul(wm_ps[:], lhsT=u3_r[:, t, :], rhs=mean_w[:], start=(t == 0), stop=(t == 3))
        wm_f = tmp.tile([P, 1], F32, name="wm_f")
        nc.vector.tensor_copy(out=wm_f[:], in_=wm_ps[:, 0:1])
        wm = keep.tile([P, 4], BF16, name="wm")
        nc.vector.memset(wm[:], 0.0)
        for k in range(3):
            nc.vector.tensor_copy(out=wm[:, k : k + 1], in_=wm_f[:])
            if k < 2:
                rest = tmp.tile([P, 1], F32, name="rest%d" % k)
                nc.vector.tensor_sub(out=rest[:], in0=wm_f[:], in1=wm[:, k : k + 1])
                wm_f = rest

        b3_f = tmp.tile([P, 4], F32, name="b3_f")
        nc.vector.tensor_copy(out=b3_f[:], in_=b3_r[:])
        bm_ps = ps_b.tile([P, 4], F32, tag="b", name="bm_ps")
        nc.tensor.matmul(bm_ps[:], lhsT=mean_f[:], rhs=b3_f[:], start=True, stop=True)
        bm = tmp.tile([P, 1], F32, name="bm")
        nc.vector.reduce_sum(out=bm[:], in_=bm_ps[:], axis=AX.X)
        b3c = keep.tile([P, 4], F32, name="b3c")
        nc.vector.tensor_scalar(out=b3c[:], in0=b3_f[:], scalar1=bm[:], scalar2=None, op0=ALU.add)

        al = tmp.tile([P, 1], F32, name="al")
        nc.vector.tensor_copy(out=al[:], in_=al_r[:])
        a3r = tmp.tile([P, 4], F32, name="a3r")
        nc.vector.tensor_scalar(out=a3r[:], in0=g3_r[:], scalar1=al[:], scalar2=None, op0=ALU.mult)
        sq = tmp.tile([P, 4], F32, name="sq")
        nc.vector.tensor_mul(out=sq[:], in0=a3r[:], in1=a3r[:])
        tiny = tmp.tile([P, 4], F32, name="tiny")
        nc.vector.tensor_scalar(out=tiny[:], in0=sq[:], scalar1=1e-24, scalar2=1e-12, op0=ALU.is_lt, op1=ALU.mult)
        a3 = tmp.tile([P, 4], F32, name="a3")
        nc.vector.tensor_add(out=a3[:], in0=a3r[:], in1=tiny[:])
        gain = keep.tile([P, 4], F32, name="gain")
        nc.vector.tensor_mul(out=gain[:], in0=a3[:], in1=g1_r[:])
        shift1 = keep.tile([P, 4], F32, name="shift1")
        nc.vector.tensor_mul(out=shift1[:], in0=a3[:], in1=e1_r[:])
        ra3 = tmp.tile([P, 4], F32, name="ra3")
        nc.vector.reciprocal(out=ra3[:], in_=a3[:])
        one3 = tmp.tile([P, 4], F32, name="one3")
        nc.vector.tensor_scalar(out=one3[:], in0=e3_r[:], scalar1=al[:], scalar2=1.0, op0=ALU.mult, op1=ALU.add)
        shift3 = keep.tile([P, 4], F32, name="shift3")
        nc.vector.tensor_mul(out=shift3[:], in0=one3[:], in1=ra3[:])

        cb_c = tmp.tile([P, 4], F32, name="cb_c")
        nc.vector.tensor_copy(out=cb_c[:], in_=cb_r[:])
        cb_ps = spread(cb_c, ps_3, "m3")
        cb = keep.tile([P, D], F32, name="cb")
        nc.scalar.copy(out=cb[:].rearrange("p (m t) -> p m t", t=4), in_=cb_ps[:].rearrange("p (t m) -> p m t", t=4))

        def st_ld(i):
            g, j = divmod(i, JT)
            if j == 0 and g >= 2:
                load(g)
                loadz(g)

        def st_x(i):
            u, k = divmod(i, 2)
            g, j = divmod(i, JT)
            if k == 0:
                state["xs", u] = sb.tile([P, 2, D], BF16, tag="xs", name="xs", bufs=6)
            nc.vector.tensor_tensor(
                out=state["xs", u][:, k, :], in0=state["xb", g][:, j * D : (j + 1) * D].bitcast(FP8), in1=xscale[:], op=ALU.mult
            )

        def st_xt(i):
            u, k = divmod(i, 2)
            if k == 0:
                return
            xs = state["xs", u]
            xp = ps_x.tile([P, 4, P], F32, tag="x", name="xp")
            for k in range(2):
                words = xs[:, k, :].bitcast(F32)
                for e in range(2):
                    nc.tensor.transpose(xp[:, 2 * k + e, :], words[:, e : D // 2 : 2], ident[:])
            state["xp", u] = xp

        def st_xe(i):
            u, k = divmod(i, 2)
            if k == 0:
                return
            xg = sb.tile([P, 2 * P * 4], BF16, tag="xg", name="xg", bufs=3, align_bytes=64)
            nc.scalar.copy(
                out=xg[:].bitcast(F32).rearrange("p (k r e) -> p k r e", k=2, e=2),
                in_=state["xp", u][:].rearrange("p (k e) r -> p k r e", k=2),
            )
            state["xg", u] = xg

        def st_qx(i):
            u, k = divmod(i, 2)
            if k == 0:
                return
            cx = sb.tile([P, 2 * P], U32, tag="cx", name="cx", bufs=6, align_bytes=64)
            sx = sb.tile([P, 2 * P], U8, tag="sx", name="sx", bufs=6, align_bytes=64)
            nc.vector.quantize_mx(out=cx[:].bitcast(FP8X4), scales=sx[:], in_=state["xg", u][:])
            state["cx", u] = (cx, sx)

        def st_m1(i):
            u, k = divmod(i, 2)
            cx, sx = state["cx", u]
            mo = ps_m.tile([P, D], F32, tag="m", name="mo1")
            nc.tensor.matmul_mx(
                out=mo[:], lhsT=cx[:, k * P : (k + 1) * P].bitcast(FP8X4), lhsT_scale=sx[:, k * P : (k + 1) * P],
                rhs=w1[:].bitcast(FP4X4), rhs_scale=w1s[:], start=True, stop=True,
            )
            state["mo1", i] = mo

        def st_y1(i):
            u, k = divmod(i, 2)
            if k == 0:
                state["sum", u] = sb.tile([P, 2], F32, tag="sum", name="sum1", bufs=12)
            y1 = sb.tile([P, D], F32, tag="y1", name="y1", bufs=12)
            nc.vector.scalar_tensor_tensor(
                out=y1[:], in0=state["mo1", i][:], scalar=1.0, in1=b1[:], op0=ALU.mult, op1=ALU.add,
                accum_out=state["sum", u][:, k : k + 1],
            )
            state["y1", i] = y1

        def st_nm1(i):
            u, k = divmod(i, 2)
            if k == 0:
                return
            nm = sb.tile([P, 2], F32, tag="nm1", name="nm1", bufs=8)
            nc.gpsimd.tensor_scalar(
                out=nm[:], in0=state["sum", u][:], scalar1=-1.0 / D, scalar2=0.0, op0=ALU.mult, op1=ALU.add
            )
            state["nm1", u] = nm

        def st_zt(i):
            g, j = divmod(i, GT)
            if j:
                return
            q, r = divmod(i, JT)
            zb = state["zb", q]
            zp = ps_x.tile([P, GT * P], BF16, tag="x", name="zp")
            for k in range(GT):
                nc.tensor.transpose(zp[:, k * P : (k + 1) * P], zb[:, (r + k) * DQ : (r + k + 1) * DQ], ident_b[:])
            state["zp", g] = zp

        def st_ze(i):
            g, j = divmod(i, GT)
            if j:
                return
            zs = sb.tile([P, GT * P], BF16, tag="zs", name="zs", bufs=3)
            nc.scalar.copy(out=zs[:], in_=state["zp", g][:])
            state["zs", g] = zs

        def st_mn(i):
            g, j = divmod(i, GT)
            if j:
                return
            mp = ps_x.tile([P, GT, 4], F32, tag="x", name="mp")
            for k in range(GT):
                nc.tensor.matmul(
                    mp[:, k, :], lhsT=state["zs", g][:, k * P : (k + 1) * P], rhs=wm[:], start=True, stop=True
                )
            state["mp", g] = mp

        def st_ng(i):
            g, j = divmod(i, GT)
            if j:
                return
            nm3 = sb.tile([P, GT], F32, tag="nm3", name="nm3", bufs=4)
            nc.vector.reduce_sum(out=nm3[:], in_=state["mp", g][:], axis=AX.X)
            state["nm3", g] = nm3

        def st_t3b(i):
            m3 = ps_3.tile([P, D], F32, tag="m3", name="m3")
            for t in range(4):
                nc.tensor.matmul(
                    m3[:, t * P : (t + 1) * P], lhsT=b3c[:, t : t + 1].to_broadcast([P, P]), rhs=ident[:],
                    start=(t == 0), stop=False, is_transpose=True,
                )
            state["m3", i] = m3

        def st_m3(i):
            g, j = divmod(i, GT)
            nc.tensor.matmul(
                state["m3", i][:], lhsT=state["zs", g][:, j * P : (j + 1) * P], rhs=u3t[:], start=False, stop=True
            )

        def get_ss(u):
            if ("ss", u) not in state:
                state["ss", u] = sb.tile([P, 4], F32, tag="ss", name="ss", bufs=10)
            return state["ss", u]

        def st_sq3(i):
            g, j = divmod(i, GT)
            u, k = divmod(i, 2)
            junk = sb.tile([P, D], BF16, tag="junk", name="junk", bufs=2)
            nc.scalar.activation(
                out=junk[:], in_=state["m3", i][:], func=ACT.Square, bias=state["nm3", g][:, j : j + 1],
                accum_out=get_ss(u)[:, 2 + k : 3 + k],
            )

        def st_sq1(i):
            u, k = divmod(i, 2)
            junk = sb.tile([P, D], BF16, tag="junk", name="junk", bufs=2)
            nc.scalar.activation(
                out=junk[:], in_=state["y1", i][:], func=ACT.Square, bias=state["nm1", u][:, k : k + 1],
                accum_out=get_ss(u)[:, k : k + 1],
            )

        def st_rs(i):
            u, k = divmod(i, 2)
            if k == 0:
                return
            sd = sb.tile([P, 4], F32, tag="sd", name="sd", bufs=6)
            nc.scalar.activation(out=sd[:], in_=state["ss", u][:], func=ACT.Sqrt, scale=1.0 / D, bias=eps[:])
            state["sd", u] = sd

        def st_rv(i):
            u, k = divmod(i, 2)
            if k == 0:
                return
            rs = sb.tile([P, 4], F32, tag="rs", name="rs", bufs=10)
            nc.vector.reciprocal(out=rs[:], in_=state["sd", u][:])
            state["rs", u] = rs

        def st_nr(i):
            u, k = divmod(i, 2)
            if k == 0:
                return
            nr = sb.tile([P, 2], F32, tag="nr", name="nr", bufs=10)
            nc.gpsimd.tensor_tensor(out=nr[:], in0=state["rs", u][:, 2:4], in1=state["nm3", u][:], op=ALU.mult)
            state["nr", u] = nr

        def st_n3(i):
            u, k = divmod(i, 2)
            n3 = sb.tile([P, D], F32, tag="n3", name="n3", bufs=12)
            nc.scalar.activation(
                out=n3[:], in_=state["m3", i][:], func=ACT.Identity, scale=state["rs", u][:, 2 + k : 3 + k],
                bias=state["nr", u][:, k : k + 1],
            )
            state["n3", i] = n3

        def st_n1(i):
            u, k = divmod(i, 2)
            n1 = sb.tile([P, D], F32, tag="n1", name="n1", bufs=12)
            nc.gpsimd.tensor_scalar(
                out=n1[:], in0=state["y1", i][:], scalar1=state["nm1", u][:, k : k + 1],
                scalar2=state["rs", u][:, k : k + 1], op0=ALU.add, op1=ALU.mult,
            )
            state["n1", i] = n1

        def c_index(i, half):
            g, k = divmod(i, 2)
            return g, 2 * k + half

        def st_t1(i, half):
            g, t = c_index(i, half)
            pa = ps_a.tile([P, GT * P], F32, tag="a", name="pa")
            for k in range(GT):
                nc.tensor.transpose(pa[:, k * P : (k + 1) * P], state["n1", g * GT + k][:, t * P : (t + 1) * P], ident[:])
            state["pa", g, t] = pa

        def st_o1(i, half):
            g, t = c_index(i, half)
            o1 = sb.tile([P, GT * P], F32, tag="o1", name="o1", bufs=4)
            nc.scalar.activation(
                out=o1[:], in_=state["pa", g, t][:], func=ACT.Identity, scale=gain[:, t : t + 1], bias=shift1[:, t : t + 1]
            )
            state["o1", g, t] = o1

        def st_t3(i, half):
            g, t = c_index(i, half)
            pb = ps_b.tile([P, GT * P], F32, tag="b", name="pb")
            for k in range(GT):
                nc.tensor.transpose(pb[:, k * P : (k + 1) * P], state["n3", g * GT + k][:, t * P : (t + 1) * P], ident[:])
            state["pb", g, t] = pb

        def st_h(i, half):
            g, t = c_index(i, half)
            if t == 0:
                state["hp", g] = sb.tile([P, 4, GT * P], BF16, tag="hp", name="hp", bufs=3)
            nc.vector.scalar_tensor_tensor(
                out=state["hp", g][:, t, :], in0=state["pb", g, t][:], scalar=shift3[:, t : t + 1], in1=state["o1", g, t][:],
                op0=ALU.add, op1=ALU.mult,
            )

        def st_il(i):
            u, k = divmod(i, 2)
            if k == 0:
                state["hi", u] = sb.tile([P, 2 * P * 4], BF16, tag="hi", name="hi", bufs=4, align_bytes=64)
            nc.gpsimd.tensor_scalar(
                out=state["hi", u][:, k * 4 * P : (k + 1) * 4 * P].rearrange("p (r t) -> p r t", t=4),
                in0=state["hp", u][:, :, k * P : (k + 1) * P].rearrange("p t r -> p r t"),
                scalar1=1.0, scalar2=0.0, op0=ALU.mult, op1=ALU.add,
            )

        def st_qh(i):
            u, k = divmod(i, 2)
            if k == 0:
                return
            ch = sb.tile([P, 2 * P], U32, tag="ch", name="ch", bufs=4, align_bytes=64)
            sh = sb.tile([P, 2 * P], U8, tag="sh", name="sh", bufs=4, align_bytes=64)
            nc.vector.quantize_mx(out=ch[:].bitcast(FP8X4), scales=sh[:], in_=state["hi", u][:])
            state["ch", u] = (ch, sh)

        def st_m2(i):
            u, k = divmod(i, 2)
            ch, sh = state["ch", u]
            mo = ps_m.tile([P, D], F32, tag="m", name="mo2")
            nc.tensor.matmul_mx(
                out=mo[:], lhsT=ch[:, k * P : (k + 1) * P].bitcast(FP8X4), lhsT_scale=sh[:, k * P : (k + 1) * P],
                rhs=cw[:].bitcast(FP4X4), rhs_scale=cws[:], start=True, stop=True,
            )
            state["mo2", i] = mo

        def st_re(i):
            u, k = divmod(i, 2)
            if k == 0:
                state["ot", u] = sb.tile([P, 2, D], F32, tag="ot", name="ot", bufs=5)
            nc.vector.tensor_tensor(out=state["ot", u][:, k, :], in0=state["mo2", i][:], in1=cb[:], op=ALU.add)

        def st_st(i):
            u, k = divmod(i, 2)
            if k == 0:
                return
            q, r = divmod(i - 1, JT)
            nc.sync.dma_start(out=ov[q][:, r * D : (r + 2) * D], in_=state["ot", u][:].rearrange("p k n -> p (k n)"))

        schedule = [
            (st_ng, -3),
            (st_m3, -3),
            (lambda i: st_o1(i, 1), 1),
            (st_rv, -2),
            (lambda i: st_t3(i, 1), 1),
            (st_sq3, -3),
            (st_qx, -5),
            (st_x, -8),
            (st_il, 3),
            (st_ld, -14),
            (st_nr, -2),
            (st_zt, -4),
            (st_m1, -4),
            (st_qh, 3),
            (lambda i: st_h(i, 1), 1),
            (st_n1, -1),
            (st_m2, 5),
            (lambda i: st_t1(i, 0), 0),
            (st_y1, -4),
            (st_n3, -1),
            (st_ze, -4),
            (lambda i: st_o1(i, 0), 0),
            (st_st, 12),
            (st_xt, -6),
            (lambda i: st_t3(i, 0), 0),
            (st_re, 5),
            (st_t3b, -4),
            (st_xe, -6),
            (lambda i: st_h(i, 0), 0),
            (st_nm1, -4),
            (st_sq1, -3),
            (st_rs, -3),
            (st_mn, -4),
            (lambda i: st_t1(i, 1), 0),
        ]
        lags = [lag for stage, lag in schedule]
        with tc.manual_schedule():
            for s in range(min(lags), NT + max(lags)):
                for stage, lag in schedule:
                    if 0 <= s - lag < NT:
                        stage(s - lag)
